import numpy as np
import ml_dtypes

BF16 = ml_dtypes.bfloat16


def bf(x):
    return np.asarray(x, np.float32).astype(BF16)


def f32(x):
    return np.asarray(x, np.float32)


def f64(x):
    return np.asarray(x).astype(np.float64)


def striped(idx):
    return np.tile(idx.reshape(-1, 16).T, (8, 1))


F, P, C, M, S, T, N, H = 16, 256, 512, 1024, 1024, 256, 512, 768


def rope_table():
    freq = f32(10000.0 ** (-np.arange(F) / F))
    ang = f32(np.arange(S))[None, :] * freq[:, None]
    reps = (P // F, 1)
    return f32(np.concatenate([np.tile(np.cos(f64(ang)), reps), np.tile(np.sin(f64(ang)), reps)], axis=0))


def setup_inputs():
    return {"tab": rope_table(), "hid": bf(np.random.standard_normal((H, T))), "w": bf(0.02 * np.random.standard_normal((H, M))), "b": f32(0.1 * np.random.standard_normal((M, 1))), "offs": striped(np.random.permutation(np.tile(np.arange(S), 2))[:N])}


def reference(tab, hid, w, b, offs):
    idx = offs[:16].T.reshape(-1)
    proj = f64(w).T @ f64(hid) + f64(b)
    v = np.concatenate([proj[:C], proj[C:]], axis=1)
    pick = f64(tab)[:, idx]
    co, si = pick[:P], pick[P:]
    ev, od = v[:P], v[P:]
    return np.concatenate([co * ev - si * od, co * od + si * ev], axis=0)

@@ -1,0 +1,103 @@
+import concourse.mybir as mybir
+from concourse.masks import make_identity
+
+F32 = mybir.dt.float32
+BF16 = mybir.dt.bfloat16
+U16 = mybir.dt.uint16
+MULT = mybir.AluOpType.mult
+ADD = mybir.AluOpType.add
+SUBTRACT = mybir.AluOpType.subtract
+IDENTITY = mybir.ActivationFunctionType.Identity
+
+P = 128
+H = 768
+KB = H // P
+T = 256
+S = 1024
+N = 2 * T
+M = 1024
+MB = M // P
+
+FLOPS = 2 * H * M * T
+
+
+def tile_globalpointermodel_kernel(tc, tab, hid, w, b, offs, out):
+    nc = tc.nc
+    with (
+        tc.tile_pool(name="held", bufs=1) as held,
+        tc.tile_pool(name="work", bufs=2) as work,
+        tc.psum_pool(name="bias_bank", bufs=1) as bias_bank,
+        tc.psum_pool(name="banks", bufs=4) as banks,
+    ):
+        offsets = held.tile([P, N // 16], U16, name="offsets")
+        nc.sync.dma_start(offsets[:], offs)
+
+        bias_rows = held.tile([MB, P], F32, name="bias_rows")
+        nc.sync.dma_start(bias_rows[:], b.rearrange("(m p) one -> m (p one)", p=P))
+
+        hid_sb = held.tile([P, KB, T], BF16, name="hid_sb")
+        nc.sync.dma_start(hid_sb[:], hid.rearrange("(p k) t -> p k t", k=KB))
+
+        w_view = w.rearrange("(p k) m -> p k m", k=KB)
+        w_half = [held.tile([P, KB, M // 2], BF16, name=f"w_half{h}") for h in range(2)]
+        table = [held.tile([P, S], F32, name=f"table{q}") for q in range(4)]
+
+        def load_w(h):
+            nc.sync.dma_start(w_half[h][:], w_view[:, :, h * (M // 2) : (h + 1) * (M // 2)])
+
+        def load_table(q):
+            nc.sync.dma_start(table[q][:], tab[q * P : (q + 1) * P, :])
+
+        load_w(0)
+        load_table(0)
+        load_table(2)
+        load_w(1)
+        load_table(1)
+        load_table(3)
+
+        identity = held.tile([MB, MB], F32, name="identity")
+        make_identity(nc, identity[:])
+        bias_ps = bias_bank.tile([P, MB], F32, name="bias_ps")
+        nc.tensor.matmul(bias_ps[:], bias_rows[:], identity[:], start=True, stop=True)
+        bias_cols = held.tile([P, MB], F32, name="bias_cols")
+        nc.scalar.activation(bias_cols[:], bias_ps[:], IDENTITY)
+
+        def project(h, c):
+            acc = banks.tile([P, T], F32, name="acc")
+            for k in range(KB):
+                nc.tensor.matmul(
+                    acc[:],
+                    w_half[h][:, k, c * P : (c + 1) * P],
+                    hid_sb[:, k, :],
+                    start=(k == 0),
+                    stop=(k == KB - 1),
+                )
+            v = work.tile([P, T], F32, name=f"v{c}")
+            m = h * (MB // 2) + c
+            nc.scalar.activation(v[:], acc[:], IDENTITY, bias=bias_cols[:, m : m + 1])
+            return v
+
+        for g in range(2):
+            cos, sin = table[g], table[2 + g]
+            for h in range(2):
+                even = project(h, g)
+                odd = project(h, 2 + g)
+                piece = offsets[:, h * (T // 16) : (h + 1) * (T // 16)]
+
+                cos_even = work.tile([P, T], F32, name="cos_even")
+                sin_odd = work.tile([P, T], F32, name="sin_odd")
+                cos_odd = work.tile([P, T], F32, name="cos_odd")
+                sin_even = work.tile([P, T], F32, name="sin_even")
+                nc.vector.tensor_tensor(cos_even[:], cos[:].indirect(piece), even[:], MULT)
+                nc.vector.tensor_tensor(cos_odd[:], cos[:].indirect(piece), odd[:], MULT)
+                nc.vector.tensor_tensor(sin_odd[:], sin[:].indirect(piece), odd[:], MULT)
+                nc.vector.tensor_tensor(sin_even[:], sin[:].indirect(piece), even[:], MULT)
+
+                top = work.tile([P, T], F32, name="top")
+                bottom = work.tile([P, T], F32, name="bottom")
+                nc.vector.tensor_tensor(top[:], cos_even[:], sin_odd[:], SUBTRACT)
+                nc.vector.tensor_tensor(bottom[:], cos_odd[:], sin_even[:], ADD)
+
+                columns = slice(h * T, (h + 1) * T)
+                nc.sync.dma_start(out[g * P : (g + 1) * P, columns], top[:])
+                nc.sync.dma_start(out[(2 + g) * P : (3 + g) * P, columns], bottom[:])

@@ -1,5 +1,4 @@
 import concourse.mybir as mybir
-from concourse.masks import make_identity
 
 F32 = mybir.dt.float32
 BF16 = mybir.dt.bfloat16
@@ -12,11 +11,14 @@ IDENTITY = mybir.ActivationFunctionType.Identity
 P = 128
 H = 768
 KB = H // P
+KC = 2
 T = 256
 S = 1024
 N = 2 * T
 M = 1024
 MB = M // P
+WARM_COLUMNS = 512
+WARM_PRODUCTS = 6
 
 FLOPS = 2 * H * M * T
 
@@ -26,24 +28,42 @@ def tile_globalpointermodel_kernel(tc, tab, hid, w, b, offs, out):
     with (
         tc.tile_pool(name="held", bufs=1) as held,
         tc.tile_pool(name="work", bufs=2) as work,
-        tc.psum_pool(name="bias_bank", bufs=1) as bias_bank,
-        tc.psum_pool(name="banks", bufs=4) as banks,
+        tc.psum_pool(name="small_banks", bufs=1) as small_banks,
+        tc.psum_pool(name="banks", bufs=3) as banks,
     ):
+        zeros = held.tile([P, WARM_COLUMNS], BF16, name="zeros")
+        nc.vector.memset(zeros[:], 0.0)
+        warm_ps = small_banks.tile([P, WARM_COLUMNS], F32, name="warm_ps")
+        for i in range(WARM_PRODUCTS):
+            nc.tensor.matmul(warm_ps[:], zeros[:, 0:P], zeros[:], start=True, stop=True)
+
+        bias_row = held.tile([1, M], F32, name="bias_row")
+        nc.sync.dma_start(bias_row[:], b.rearrange("m one -> one m"))
+        one = held.tile([1, 1], F32, name="one")
+        nc.vector.memset(one[:], 1.0)
+        bias_ps = small_banks.tile([P, MB], F32, name="bias_ps")
+        for m in range(MB):
+            nc.tensor.matmul(bias_ps[:, m : m + 1], bias_row[:, m * P : (m + 1) * P], one[:], start=True, stop=True)
+        bias_cols = held.tile([P, MB], F32, name="bias_cols")
+        nc.scalar.activation(bias_cols[:], bias_ps[:], IDENTITY)
+
         offsets = held.tile([P, N // 16], U16, name="offsets")
         nc.sync.dma_start(offsets[:], offs)
-
-        bias_rows = held.tile([MB, P], F32, name="bias_rows")
-        nc.sync.dma_start(bias_rows[:], b.rearrange("(m p) one -> m (p one)", p=P))
 
         hid_sb = held.tile([P, KB, T], BF16, name="hid_sb")
         nc.sync.dma_start(hid_sb[:], hid.rearrange("(p k) t -> p k t", k=KB))
 
         w_view = w.rearrange("(p k) m -> p k m", k=KB)
-        w_half = [held.tile([P, KB, M // 2], BF16, name=f"w_half{h}") for h in range(2)]
+        w_part = [
+            [held.tile([P, KC, M // 2], BF16, name=f"w_part{h}_{i}") for i in range(KB // KC)] for h in range(2)
+        ]
         table = [held.tile([P, S], F32, name=f"table{q}") for q in range(4)]
 
         def load_w(h):
-            nc.sync.dma_start(w_half[h][:], w_view[:, :, h * (M // 2) : (h + 1) * (M // 2)])
+            for i in range(KB // KC):
+                nc.sync.dma_start(
+                    w_part[h][i][:], w_view[:, i * KC : (i + 1) * KC, h * (M // 2) : (h + 1) * (M // 2)]
+                )
 
         def load_table(q):
             nc.sync.dma_start(table[q][:], tab[q * P : (q + 1) * P, :])
@@ -55,33 +75,30 @@ def tile_globalpointermodel_kernel(tc, tab, hid, w, b, offs, out):
         load_table(1)
         load_table(3)
 
-        identity = held.tile([MB, MB], F32, name="identity")
-        make_identity(nc, identity[:])
-        bias_ps = bias_bank.tile([P, MB], F32, name="bias_ps")
-        nc.tensor.matmul(bias_ps[:], bias_rows[:], identity[:], start=True, stop=True)
-        bias_cols = held.tile([P, MB], F32, name="bias_cols")
-        nc.scalar.activation(bias_cols[:], bias_ps[:], IDENTITY)
-
-        def project(h, c):
-            acc = banks.tile([P, T], F32, name="acc")
+        def project_pair(h, g):
+            accs = [banks.tile([P, T], F32, name=f"acc{member}") for member in range(2)]
             for k in range(KB):
-                nc.tensor.matmul(
-                    acc[:],
-                    w_half[h][:, k, c * P : (c + 1) * P],
-                    hid_sb[:, k, :],
-                    start=(k == 0),
-                    stop=(k == KB - 1),
-                )
-            v = work.tile([P, T], F32, name=f"v{c}")
-            m = h * (MB // 2) + c
-            nc.scalar.activation(v[:], acc[:], IDENTITY, bias=bias_cols[:, m : m + 1])
-            return v
+                for member in range(2):
+                    c = 2 * member + g
+                    nc.tensor.matmul(
+                        accs[member][:],
+                        w_part[h][k // KC][:, k % KC, c * P : (c + 1) * P],
+                        hid_sb[:, k, :],
+                        start=(k == 0),
+                        stop=(k == KB - 1),
+                    )
+            members = []
+            for member in range(2):
+                m = h * (MB // 2) + 2 * member + g
+                v = work.tile([P, T], F32, name=f"v{member}")
+                nc.scalar.activation(v[:], accs[member][:], IDENTITY, bias=bias_cols[:, m : m + 1])
+                members.append(v)
+            return members
 
         for g in range(2):
             cos, sin = table[g], table[2 + g]
             for h in range(2):
-                even = project(h, g)
-                odd = project(h, 2 + g)
+                even, odd = project_pair(h, g)
                 piece = offsets[:, h * (T // 16) : (h + 1) * (T // 16)]
 
                 cos_even = work.tile([P, T], F32, name="cos_even")

@@ -28,24 +28,23 @@ def tile_globalpointermodel_kernel(tc, tab, hid, w, b, offs, out):
     with (
         tc.tile_pool(name="held", bufs=1) as held,
         tc.tile_pool(name="work", bufs=2) as work,
-        tc.psum_pool(name="small_banks", bufs=1) as small_banks,
+        tc.psum_pool(name="warm_bank", bufs=1) as warm_bank,
         tc.psum_pool(name="banks", bufs=3) as banks,
     ):
         zeros = held.tile([P, WARM_COLUMNS], BF16, name="zeros")
         nc.vector.memset(zeros[:], 0.0)
-        warm_ps = small_banks.tile([P, WARM_COLUMNS], F32, name="warm_ps")
+        warm_ps = warm_bank.tile([P, WARM_COLUMNS], F32, name="warm_ps")
         for i in range(WARM_PRODUCTS):
             nc.tensor.matmul(warm_ps[:], zeros[:, 0:P], zeros[:], start=True, stop=True)
 
-        bias_row = held.tile([1, M], F32, name="bias_row")
-        nc.sync.dma_start(bias_row[:], b.rearrange("m one -> one m"))
-        one = held.tile([1, 1], F32, name="one")
-        nc.vector.memset(one[:], 1.0)
-        bias_ps = small_banks.tile([P, MB], F32, name="bias_ps")
-        for m in range(MB):
-            nc.tensor.matmul(bias_ps[:, m : m + 1], bias_row[:, m * P : (m + 1) * P], one[:], start=True, stop=True)
         bias_cols = held.tile([P, MB], F32, name="bias_cols")
-        nc.scalar.activation(bias_cols[:], bias_ps[:], IDENTITY)
+        with nc.allow_non_contiguous_dma(reason="the bias goes one value to a partition"):
+            nc.scalar.dma_start(bias_cols[:], b.rearrange("(m p) one -> p (m one)", p=P))
+
+        nothing = held.tile([P, 1], F32, name="nothing")
+        nc.vector.memset(nothing[:], 0.0)
+        still_nothing = held.tile([P, 1], F32, name="still_nothing")
+        nc.scalar.activation(still_nothing[:], nothing[:], IDENTITY)
 
         offsets = held.tile([P, N // 16], U16, name="offsets")
         nc.sync.dma_start(offsets[:], offs)
@@ -71,9 +70,9 @@ def tile_globalpointermodel_kernel(tc, tab, hid, w, b, offs, out):
         load_w(0)
         load_table(0)
         load_table(2)
-        load_w(1)
         load_table(1)
         load_table(3)
+        load_w(1)
 
         def project_pair(h, g):
             accs = [banks.tile([P, T], F32, name=f"acc{member}") for member in range(2)]
@@ -95,11 +94,12 @@ def tile_globalpointermodel_kernel(tc, tab, hid, w, b, offs, out):
                 members.append(v)
             return members
 
-        for g in range(2):
-            cos, sin = table[g], table[2 + g]
-            for h in range(2):
+        for h in range(2):
+            piece = offsets[:, h * (T // 16) : (h + 1) * (T // 16)]
+            columns = slice(h * T, (h + 1) * T)
+            for g in range(2):
+                cos, sin = table[g], table[2 + g]
                 even, odd = project_pair(h, g)
-                piece = offsets[:, h * (T // 16) : (h + 1) * (T // 16)]
 
                 cos_even = work.tile([P, T], F32, name="cos_even")
                 sin_odd = work.tile([P, T], F32, name="sin_odd")
@@ -115,6 +115,5 @@ def tile_globalpointermodel_kernel(tc, tab, hid, w, b, offs, out):
                 nc.vector.tensor_tensor(top[:], cos_even[:], sin_odd[:], SUBTRACT)
                 nc.vector.tensor_tensor(bottom[:], cos_odd[:], sin_even[:], ADD)
 
-                columns = slice(h * T, (h + 1) * T)
                 nc.sync.dma_start(out[g * P : (g + 1) * P, columns], top[:])
                 nc.sync.dma_start(out[(2 + g) * P : (3 + g) * P, columns], bottom[:])

@@ -16,7 +16,6 @@ T = 256
 S = 1024
 N = 2 * T
 M = 1024
-MB = M // P
 WARM_COLUMNS = 512
 WARM_PRODUCTS = 6
 
@@ -37,9 +36,12 @@ def tile_globalpointermodel_kernel(tc, tab, hid, w, b, offs, out):
         for i in range(WARM_PRODUCTS):
             nc.tensor.matmul(warm_ps[:], zeros[:, 0:P], zeros[:], start=True, stop=True)
 
-        bias_cols = held.tile([P, MB], F32, name="bias_cols")
+        b_view = b.rearrange("(h member g p) one -> p h g (member one)", h=2, member=2, g=2)
+        bias_pair = [[held.tile([P, 2], F32, name=f"bias_pair{h}{g}") for g in range(2)] for h in range(2)]
         with nc.allow_non_contiguous_dma(reason="the bias goes one value to a partition"):
-            nc.scalar.dma_start(bias_cols[:], b.rearrange("(m p) one -> p (m one)", p=P))
+            for h in range(2):
+                for g in range(2):
+                    nc.scalar.dma_start(bias_pair[h][g][:], b_view[:, h, g, :])
 
         nothing = held.tile([P, 1], F32, name="nothing")
         nc.vector.memset(nothing[:], 0.0)
@@ -88,9 +90,8 @@ def tile_globalpointermodel_kernel(tc, tab, hid, w, b, offs, out):
                     )
             members = []
             for member in range(2):
-                m = h * (MB // 2) + 2 * member + g
                 v = work.tile([P, T], F32, name=f"v{member}")
-                nc.scalar.activation(v[:], accs[member][:], IDENTITY, bias=bias_cols[:, m : m + 1])
+                nc.scalar.activation(v[:], accs[member][:], IDENTITY, bias=bias_pair[h][g][:, member : member + 1])
                 members.append(v)
             return members
 

@@ -28,7 +28,7 @@ def tile_globalpointermodel_kernel(tc, tab, hid, w, b, offs, out):
         tc.tile_pool(name="held", bufs=1) as held,
         tc.tile_pool(name="work", bufs=2) as work,
         tc.psum_pool(name="warm_bank", bufs=1) as warm_bank,
-        tc.psum_pool(name="banks", bufs=3) as banks,
+        tc.psum_pool(name="banks", bufs=2) as banks,
     ):
         zeros = held.tile([P, WARM_COLUMNS], BF16, name="zeros")
         nc.vector.memset(zeros[:], 0.0)
@@ -36,12 +36,12 @@ def tile_globalpointermodel_kernel(tc, tab, hid, w, b, offs, out):
         for i in range(WARM_PRODUCTS):
             nc.tensor.matmul(warm_ps[:], zeros[:, 0:P], zeros[:], start=True, stop=True)
 
-        b_view = b.rearrange("(h member g p) one -> p h g (member one)", h=2, member=2, g=2)
-        bias_pair = [[held.tile([P, 2], F32, name=f"bias_pair{h}{g}") for g in range(2)] for h in range(2)]
+        b_view = b.rearrange("(h member g p) one -> p g member (h one)", h=2, member=2, g=2)
+        bias_of = [[held.tile([P, 2], F32, name=f"bias_of{g}{member}") for member in range(2)] for g in range(2)]
         with nc.allow_non_contiguous_dma(reason="the bias goes one value to a partition"):
-            for h in range(2):
-                for g in range(2):
-                    nc.scalar.dma_start(bias_pair[h][g][:], b_view[:, h, g, :])
+            for g in range(2):
+                for member in range(2):
+                    nc.scalar.dma_start(bias_of[g][member][:], b_view[:, g, member, :])
 
         nothing = held.tile([P, 1], F32, name="nothing")
         nc.vector.memset(nothing[:], 0.0)
@@ -55,66 +55,51 @@ def tile_globalpointermodel_kernel(tc, tab, hid, w, b, offs, out):
         nc.sync.dma_start(hid_sb[:], hid.rearrange("(p k) t -> p k t", k=KB))
 
         w_view = w.rearrange("(p k) m -> p k m", k=KB)
-        w_part = [
-            [held.tile([P, KC, M // 2], BF16, name=f"w_part{h}_{i}") for i in range(KB // KC)] for h in range(2)
-        ]
+        w_part = [held.tile([P, KC, M], BF16, name=f"w_part{i}") for i in range(KB // KC)]
+        for i in range(KB // KC):
+            nc.sync.dma_start(w_part[i][:], w_view[:, i * KC : (i + 1) * KC, :])
+
         table = [held.tile([P, S], F32, name=f"table{q}") for q in range(4)]
-
-        def load_w(h):
-            for i in range(KB // KC):
-                nc.sync.dma_start(
-                    w_part[h][i][:], w_view[:, i * KC : (i + 1) * KC, h * (M // 2) : (h + 1) * (M // 2)]
-                )
-
-        def load_table(q):
+        for q in (0, 2, 1, 3):
             nc.sync.dma_start(table[q][:], tab[q * P : (q + 1) * P, :])
 
-        load_w(0)
-        load_table(0)
-        load_table(2)
-        load_table(1)
-        load_table(3)
-        load_w(1)
-
-        def project_pair(h, g):
-            accs = [banks.tile([P, T], F32, name=f"acc{member}") for member in range(2)]
+        def project(member, g):
+            c = 2 * member + g
+            accs = [banks.tile([P, T], F32, name=f"acc{h}") for h in range(2)]
             for k in range(KB):
-                for member in range(2):
-                    c = 2 * member + g
+                for h in range(2):
+                    first = h * (M // 2) + c * P
                     nc.tensor.matmul(
-                        accs[member][:],
-                        w_part[h][k // KC][:, k % KC, c * P : (c + 1) * P],
+                        accs[h][:],
+                        w_part[k // KC][:, k % KC, first : first + P],
                         hid_sb[:, k, :],
                         start=(k == 0),
                         stop=(k == KB - 1),
                     )
-            members = []
-            for member in range(2):
-                v = work.tile([P, T], F32, name=f"v{member}")
-                nc.scalar.activation(v[:], accs[member][:], IDENTITY, bias=bias_pair[h][g][:, member : member + 1])
-                members.append(v)
-            return members
+            v = work.tile([P, N], F32, name=f"v{member}")
+            for h in range(2):
+                nc.scalar.activation(
+                    v[:, h * T : (h + 1) * T], accs[h][:], IDENTITY, bias=bias_of[g][member][:, h : h + 1]
+                )
+            return v
 
-        for h in range(2):
-            piece = offsets[:, h * (T // 16) : (h + 1) * (T // 16)]
-            columns = slice(h * T, (h + 1) * T)
-            for g in range(2):
-                cos, sin = table[g], table[2 + g]
-                even, odd = project_pair(h, g)
+        for g in range(2):
+            cos, sin = table[g], table[2 + g]
+            even = project(0, g)
+            odd = project(1, g)
 
-                cos_even = work.tile([P, T], F32, name="cos_even")
-                sin_odd = work.tile([P, T], F32, name="sin_odd")
-                cos_odd = work.tile([P, T], F32, name="cos_odd")
-                sin_even = work.tile([P, T], F32, name="sin_even")
-                nc.vector.tensor_tensor(cos_even[:], cos[:].indirect(piece), even[:], MULT)
-                nc.vector.tensor_tensor(cos_odd[:], cos[:].indirect(piece), odd[:], MULT)
-                nc.vector.tensor_tensor(sin_odd[:], sin[:].indirect(piece), odd[:], MULT)
-                nc.vector.tensor_tensor(sin_even[:], sin[:].indirect(piece), even[:], MULT)
+            cos_even = work.tile([P, N], F32, name="cos_even")
+            sin_even = work.tile([P, N], F32, name="sin_even")
+            cos_odd = work.tile([P, N], F32, name="cos_odd")
+            sin_odd = work.tile([P, N], F32, name="sin_odd")
+            top = work.tile([P, N], F32, name="top")
+            bottom = work.tile([P, N], F32, name="bottom")
 
-                top = work.tile([P, T], F32, name="top")
-                bottom = work.tile([P, T], F32, name="bottom")
-                nc.vector.tensor_tensor(top[:], cos_even[:], sin_odd[:], SUBTRACT)
-                nc.vector.tensor_tensor(bottom[:], cos_odd[:], sin_even[:], ADD)
-
-                nc.sync.dma_start(out[g * P : (g + 1) * P, columns], top[:])
-                nc.sync.dma_start(out[(2 + g) * P : (3 + g) * P, columns], bottom[:])
+            nc.vector.tensor_tensor(cos_even[:], cos[:].indirect(offsets[:]), even[:], MULT)
+            nc.vector.tensor_tensor(sin_even[:], sin[:].indirect(offsets[:]), even[:], MULT)
+            nc.vector.tensor_tensor(cos_odd[:], cos[:].indirect(offsets[:]), odd[:], MULT)
+            nc.vector.tensor_tensor(bottom[:], cos_odd[:], sin_even[:], ADD)
+            nc.sync.dma_start(out[(2 + g) * P : (3 + g) * P, :], bottom[:])
+            nc.vector.tensor_tensor(sin_odd[:], sin[:].indirect(offsets[:]), odd[:], MULT)
+            nc.vector.tensor_tensor(top[:], cos_even[:], sin_odd[:], SUBTRACT)
+            nc.sync.dma_start(out[g * P : (g + 1) * P, :], top[:])

@@ -1,4 +1,5 @@
 import concourse.mybir as mybir
+from concourse.masks import make_identity
 
 F32 = mybir.dt.float32
 BF16 = mybir.dt.bfloat16
@@ -16,6 +17,7 @@ T = 256
 S = 1024
 N = 2 * T
 M = 1024
+MB = M // P
 WARM_COLUMNS = 512
 WARM_PRODUCTS = 6
 
@@ -27,26 +29,23 @@ def tile_globalpointermodel_kernel(tc, tab, hid, w, b, offs, out):
     with (
         tc.tile_pool(name="held", bufs=1) as held,
         tc.tile_pool(name="work", bufs=2) as work,
-        tc.psum_pool(name="warm_bank", bufs=1) as warm_bank,
-        tc.psum_pool(name="banks", bufs=2) as banks,
+        tc.psum_pool(name="small_banks", bufs=1) as small_banks,
+        tc.psum_pool(name="banks", bufs=1) as banks,
     ):
+        bias_rows = held.tile([MB, P], F32, name="bias_rows")
+        nc.sync.dma_start(bias_rows[:], b.rearrange("(m p) one -> m (p one)", p=P))
+        identity = held.tile([MB, MB], F32, name="identity")
+        make_identity(nc, identity[:])
+        bias_ps = small_banks.tile([P, MB], F32, name="bias_ps")
+        nc.tensor.matmul(bias_ps[:], bias_rows[:], identity[:], start=True, stop=True)
+        bias_cols = held.tile([P, MB], F32, name="bias_cols")
+        nc.scalar.activation(bias_cols[:], bias_ps[:], IDENTITY)
+
         zeros = held.tile([P, WARM_COLUMNS], BF16, name="zeros")
         nc.vector.memset(zeros[:], 0.0)
-        warm_ps = warm_bank.tile([P, WARM_COLUMNS], F32, name="warm_ps")
+        warm_ps = small_banks.tile([P, WARM_COLUMNS], F32, name="warm_ps")
         for i in range(WARM_PRODUCTS):
             nc.tensor.matmul(warm_ps[:], zeros[:, 0:P], zeros[:], start=True, stop=True)
-
-        b_view = b.rearrange("(h member g p) one -> p g member (h one)", h=2, member=2, g=2)
-        bias_of = [[held.tile([P, 2], F32, name=f"bias_of{g}{member}") for member in range(2)] for g in range(2)]
-        with nc.allow_non_contiguous_dma(reason="the bias goes one value to a partition"):
-            for g in range(2):
-                for member in range(2):
-                    nc.scalar.dma_start(bias_of[g][member][:], b_view[:, g, member, :])
-
-        nothing = held.tile([P, 1], F32, name="nothing")
-        nc.vector.memset(nothing[:], 0.0)
-        still_nothing = held.tile([P, 1], F32, name="still_nothing")
-        nc.scalar.activation(still_nothing[:], nothing[:], IDENTITY)
 
         offsets = held.tile([P, N // 16], U16, name="offsets")
         nc.sync.dma_start(offsets[:], offs)
@@ -55,51 +54,67 @@ def tile_globalpointermodel_kernel(tc, tab, hid, w, b, offs, out):
         nc.sync.dma_start(hid_sb[:], hid.rearrange("(p k) t -> p k t", k=KB))
 
         w_view = w.rearrange("(p k) m -> p k m", k=KB)
-        w_part = [held.tile([P, KC, M], BF16, name=f"w_part{i}") for i in range(KB // KC)]
-        for i in range(KB // KC):
-            nc.sync.dma_start(w_part[i][:], w_view[:, i * KC : (i + 1) * KC, :])
-
+        w_part = [
+            [held.tile([P, KC, M // 2], BF16, name=f"w_part{h}_{i}") for i in range(KB // KC)] for h in range(2)
+        ]
         table = [held.tile([P, S], F32, name=f"table{q}") for q in range(4)]
-        for q in (0, 2, 1, 3):
+
+        def load_w(h):
+            for i in range(KB // KC):
+                nc.sync.dma_start(
+                    w_part[h][i][:], w_view[:, i * KC : (i + 1) * KC, h * (M // 2) : (h + 1) * (M // 2)]
+                )
+
+        def load_table(q):
             nc.sync.dma_start(table[q][:], tab[q * P : (q + 1) * P, :])
 
-        def project(member, g):
-            c = 2 * member + g
-            accs = [banks.tile([P, T], F32, name=f"acc{h}") for h in range(2)]
+        load_w(0)
+        load_table(0)
+        load_table(2)
+        load_table(1)
+        load_table(3)
+        load_w(1)
+
+        def project_pair(h, g):
+            accs = [banks.tile([P, T], F32, name=f"acc{member}") for member in range(2)]
             for k in range(KB):
-                for h in range(2):
-                    first = h * (M // 2) + c * P
+                for member in range(2):
+                    c = 2 * member + g
                     nc.tensor.matmul(
-                        accs[h][:],
-                        w_part[k // KC][:, k % KC, first : first + P],
+                        accs[member][:],
+                        w_part[h][k // KC][:, k % KC, c * P : (c + 1) * P],
                         hid_sb[:, k, :],
                         start=(k == 0),
                         stop=(k == KB - 1),
                     )
-            v = work.tile([P, N], F32, name=f"v{member}")
-            for h in range(2):
-                nc.scalar.activation(
-                    v[:, h * T : (h + 1) * T], accs[h][:], IDENTITY, bias=bias_of[g][member][:, h : h + 1]
-                )
-            return v
+            members = []
+            for member in range(2):
+                m = h * (MB // 2) + 2 * member + g
+                v = work.tile([P, T], F32, name=f"v{member}")
+                nc.scalar.activation(v[:], accs[member][:], IDENTITY, bias=bias_cols[:, m : m + 1])
+                members.append(v)
+            return members
 
-        for g in range(2):
-            cos, sin = table[g], table[2 + g]
-            even = project(0, g)
-            odd = project(1, g)
+        for h in range(2):
+            piece = offsets[:, h * (T // 16) : (h + 1) * (T // 16)]
+            columns = slice(h * T, (h + 1) * T)
+            for g in range(2):
+                cos, sin = table[g], table[2 + g]
+                even, odd = project_pair(h, g)
 
-            cos_even = work.tile([P, N], F32, name="cos_even")
-            sin_even = work.tile([P, N], F32, name="sin_even")
-            cos_odd = work.tile([P, N], F32, name="cos_odd")
-            sin_odd = work.tile([P, N], F32, name="sin_odd")
-            top = work.tile([P, N], F32, name="top")
-            bottom = work.tile([P, N], F32, name="bottom")
+                cos_even = work.tile([P, T], F32, name="cos_even")
+                sin_odd = work.tile([P, T], F32, name="sin_odd")
+                cos_odd = work.tile([P, T], F32, name="cos_odd")
+                sin_even = work.tile([P, T], F32, name="sin_even")
+                nc.vector.tensor_tensor(cos_even[:], cos[:].indirect(piece), even[:], MULT)
+                nc.vector.tensor_tensor(cos_odd[:], cos[:].indirect(piece), odd[:], MULT)
+                nc.vector.tensor_tensor(sin_odd[:], sin[:].indirect(piece), odd[:], MULT)
+                nc.vector.tensor_tensor(sin_even[:], sin[:].indirect(piece), even[:], MULT)
 
-            nc.vector.tensor_tensor(cos_even[:], cos[:].indirect(offsets[:]), even[:], MULT)
-            nc.vector.tensor_tensor(sin_even[:], sin[:].indirect(offsets[:]), even[:], MULT)
-            nc.vector.tensor_tensor(cos_odd[:], cos[:].indirect(offsets[:]), odd[:], MULT)
-            nc.vector.tensor_tensor(bottom[:], cos_odd[:], sin_even[:], ADD)
-            nc.sync.dma_start(out[(2 + g) * P : (3 + g) * P, :], bottom[:])
-            nc.vector.tensor_tensor(sin_odd[:], sin[:].indirect(offsets[:]), odd[:], MULT)
-            nc.vector.tensor_tensor(top[:], cos_even[:], sin_odd[:], SUBTRACT)
-            nc.sync.dma_start(out[g * P : (g + 1) * P, :], top[:])
+                top = work.tile([P, T], F32, name="top")
+                bottom = work.tile([P, T], F32, name="bottom")
+                nc.vector.tensor_tensor(top[:], cos_even[:], sin_odd[:], SUBTRACT)
+                nc.vector.tensor_tensor(bottom[:], cos_odd[:], sin_even[:], ADD)
+
+                nc.sync.dma_start(out[g * P : (g + 1) * P, columns], top[:])
+                nc.sync.dma_start(out[(2 + g) * P : (3 + g) * P, columns], bottom[:])

@@ -31,15 +31,18 @@ def tile_globalpointermodel_kernel(tc, tab, hid, w, b, offs, out):
         tc.tile_pool(name="work", bufs=2) as work,
         tc.psum_pool(name="small_banks", bufs=1) as small_banks,
         tc.psum_pool(name="banks", bufs=1) as banks,
+        tc.psum_pool(name="sum_banks", bufs=1) as sum_banks,
     ):
         bias_rows = held.tile([MB, P], F32, name="bias_rows")
         nc.sync.dma_start(bias_rows[:], b.rearrange("(m p) one -> m (p one)", p=P))
-        identity = held.tile([MB, MB], F32, name="identity")
+        identity = held.tile([P, P], F32, name="identity")
         make_identity(nc, identity[:])
         bias_ps = small_banks.tile([P, MB], F32, name="bias_ps")
-        nc.tensor.matmul(bias_ps[:], bias_rows[:], identity[:], start=True, stop=True)
+        nc.tensor.matmul(bias_ps[:], bias_rows[:], identity[0:MB, 0:MB], start=True, stop=True)
         bias_cols = held.tile([P, MB], F32, name="bias_cols")
         nc.scalar.activation(bias_cols[:], bias_ps[:], IDENTITY)
+        minus_identity = held.tile([P, P], F32, name="minus_identity")
+        nc.scalar.mul(minus_identity[:], identity[:], -1.0)
 
         zeros = held.tile([P, WARM_COLUMNS], BF16, name="zeros")
         nc.vector.memset(zeros[:], 0.0)
@@ -95,26 +98,43 @@ def tile_globalpointermodel_kernel(tc, tab, hid, w, b, offs, out):
                 members.append(v)
             return members
 
-        for h in range(2):
+        units = [(h, g) for h in range(2) for g in range(2)]
+        projected = project_pair(*units[0])
+        for u, (h, g) in enumerate(units):
             piece = offsets[:, h * (T // 16) : (h + 1) * (T // 16)]
             columns = slice(h * T, (h + 1) * T)
-            for g in range(2):
-                cos, sin = table[g], table[2 + g]
-                even, odd = project_pair(h, g)
+            cos, sin = table[g], table[2 + g]
+            even, odd = projected
+            if u + 1 < len(units):
+                projected = project_pair(*units[u + 1])
 
-                cos_even = work.tile([P, T], F32, name="cos_even")
-                sin_odd = work.tile([P, T], F32, name="sin_odd")
-                cos_odd = work.tile([P, T], F32, name="cos_odd")
-                sin_even = work.tile([P, T], F32, name="sin_even")
-                nc.vector.tensor_tensor(cos_even[:], cos[:].indirect(piece), even[:], MULT)
-                nc.vector.tensor_tensor(cos_odd[:], cos[:].indirect(piece), odd[:], MULT)
-                nc.vector.tensor_tensor(sin_odd[:], sin[:].indirect(piece), odd[:], MULT)
-                nc.vector.tensor_tensor(sin_even[:], sin[:].indirect(piece), even[:], MULT)
+            cos_even = work.tile([P, T], F32, name="cos_even")
+            sin_odd = work.tile([P, T], F32, name="sin_odd")
+            cos_odd = work.tile([P, T], F32, name="cos_odd")
+            sin_even = work.tile([P, T], F32, name="sin_even")
+            nc.vector.tensor_tensor(cos_even[:], cos[:].indirect(piece), even[:], MULT)
+            nc.vector.tensor_tensor(cos_odd[:], cos[:].indirect(piece), odd[:], MULT)
+            nc.vector.tensor_tensor(sin_odd[:], sin[:].indirect(piece), odd[:], MULT)
+            nc.vector.tensor_tensor(sin_even[:], sin[:].indirect(piece), even[:], MULT)
 
-                top = work.tile([P, T], F32, name="top")
-                bottom = work.tile([P, T], F32, name="bottom")
+            top = work.tile([P, T], F32, name="top")
+            bottom = work.tile([P, T], F32, name="bottom")
+            tensor_adds_top = g == 0
+            tensor_adds_bottom = u == len(units) - 2
+            if tensor_adds_top:
+                top_ps = sum_banks.tile([P, T], F32, name="top_ps")
+                nc.tensor.matmul(top_ps[:], identity[:], cos_even[:], start=True, stop=False)
+                nc.tensor.matmul(top_ps[:], minus_identity[:], sin_odd[:], start=False, stop=True)
+                nc.scalar.activation(top[:], top_ps[:], IDENTITY)
+            else:
                 nc.vector.tensor_tensor(top[:], cos_even[:], sin_odd[:], SUBTRACT)
+            if tensor_adds_bottom:
+                bottom_ps = sum_banks.tile([P, T], F32, name="bottom_ps")
+                nc.tensor.matmul(bottom_ps[:], identity[:], cos_odd[:], start=True, stop=False)
+                nc.tensor.matmul(bottom_ps[:], identity[:], sin_even[:], start=False, stop=True)
+                nc.scalar.activation(bottom[:], bottom_ps[:], IDENTITY)
+            else:
                 nc.vector.tensor_tensor(bottom[:], cos_odd[:], sin_even[:], ADD)
 
-                nc.sync.dma_start(out[g * P : (g + 1) * P, columns], top[:])
-                nc.sync.dma_start(out[(2 + g) * P : (3 + g) * P, columns], bottom[:])
+            nc.sync.dma_start(out[g * P : (g + 1) * P, columns], top[:])
+            nc.sync.dma_start(out[(2 + g) * P : (3 + g) * P, columns], bottom[:])

@@ -119,22 +119,14 @@ def tile_globalpointermodel_kernel(tc, tab, hid, w, b, offs, out):
 
             top = work.tile([P, T], F32, name="top")
             bottom = work.tile([P, T], F32, name="bottom")
-            tensor_adds_top = g == 0
-            tensor_adds_bottom = u == len(units) - 2
-            if tensor_adds_top:
+            if g == 0:
                 top_ps = sum_banks.tile([P, T], F32, name="top_ps")
                 nc.tensor.matmul(top_ps[:], identity[:], cos_even[:], start=True, stop=False)
                 nc.tensor.matmul(top_ps[:], minus_identity[:], sin_odd[:], start=False, stop=True)
                 nc.scalar.activation(top[:], top_ps[:], IDENTITY)
             else:
                 nc.vector.tensor_tensor(top[:], cos_even[:], sin_odd[:], SUBTRACT)
-            if tensor_adds_bottom:
-                bottom_ps = sum_banks.tile([P, T], F32, name="bottom_ps")
-                nc.tensor.matmul(bottom_ps[:], identity[:], cos_odd[:], start=True, stop=False)
-                nc.tensor.matmul(bottom_ps[:], identity[:], sin_even[:], start=False, stop=True)
-                nc.scalar.activation(bottom[:], bottom_ps[:], IDENTITY)
-            else:
-                nc.vector.tensor_tensor(bottom[:], cos_odd[:], sin_even[:], ADD)
+            nc.vector.tensor_tensor(bottom[:], cos_odd[:], sin_even[:], ADD)
 
             nc.sync.dma_start(out[g * P : (g + 1) * P, columns], top[:])
             nc.sync.dma_start(out[(2 + g) * P : (3 + g) * P, columns], bottom[:])

@@ -35,14 +35,12 @@ def tile_globalpointermodel_kernel(tc, tab, hid, w, b, offs, out):
     ):
         bias_rows = held.tile([MB, P], F32, name="bias_rows")
         nc.sync.dma_start(bias_rows[:], b.rearrange("(m p) one -> m (p one)", p=P))
-        identity = held.tile([P, P], F32, name="identity")
-        make_identity(nc, identity[:])
+        small_identity = held.tile([MB, MB], F32, name="small_identity")
+        make_identity(nc, small_identity[:])
         bias_ps = small_banks.tile([P, MB], F32, name="bias_ps")
-        nc.tensor.matmul(bias_ps[:], bias_rows[:], identity[0:MB, 0:MB], start=True, stop=True)
+        nc.tensor.matmul(bias_ps[:], bias_rows[:], small_identity[:], start=True, stop=True)
         bias_cols = held.tile([P, MB], F32, name="bias_cols")
         nc.scalar.activation(bias_cols[:], bias_ps[:], IDENTITY)
-        minus_identity = held.tile([P, P], F32, name="minus_identity")
-        nc.scalar.mul(minus_identity[:], identity[:], -1.0)
 
         zeros = held.tile([P, WARM_COLUMNS], BF16, name="zeros")
         nc.vector.memset(zeros[:], 0.0)
@@ -77,6 +75,11 @@ def tile_globalpointermodel_kernel(tc, tab, hid, w, b, offs, out):
         load_table(1)
         load_table(3)
         load_w(1)
+
+        identity = held.tile([P, P], F32, name="identity")
+        make_identity(nc, identity[:])
+        minus_identity = held.tile([P, P], F32, name="minus_identity")
+        nc.scalar.mul(minus_identity[:], identity[:], -1.0)
 
         def project_pair(h, g):
             accs = [banks.tile([P, T], F32, name=f"acc{member}") for member in range(2)]

@@ -18,6 +18,7 @@ S = 1024
 N = 2 * T
 M = 1024
 MB = M // P
+SQUARE = 32
 WARM_COLUMNS = 512
 WARM_PRODUCTS = 6
 
@@ -33,14 +34,13 @@ def tile_globalpointermodel_kernel(tc, tab, hid, w, b, offs, out):
         tc.psum_pool(name="banks", bufs=1) as banks,
         tc.psum_pool(name="sum_banks", bufs=1) as sum_banks,
     ):
-        bias_rows = held.tile([MB, P], F32, name="bias_rows")
-        nc.sync.dma_start(bias_rows[:], b.rearrange("(m p) one -> m (p one)", p=P))
-        small_identity = held.tile([MB, MB], F32, name="small_identity")
-        make_identity(nc, small_identity[:])
-        bias_ps = small_banks.tile([P, MB], F32, name="bias_ps")
-        nc.tensor.matmul(bias_ps[:], bias_rows[:], small_identity[:], start=True, stop=True)
-        bias_cols = held.tile([P, MB], F32, name="bias_cols")
-        nc.scalar.activation(bias_cols[:], bias_ps[:], IDENTITY)
+        bias_rows = held.tile([P, SQUARE], F32, name="bias_rows", align_bytes=64)
+        nc.vector.memset(bias_rows[:], 0.0)
+        b_view = b.rearrange("(m q i) one -> q m (i one)", q=P // SQUARE, i=SQUARE)
+        for q in range(P // SQUARE):
+            nc.scalar.dma_start(bias_rows[q * SQUARE : q * SQUARE + MB, :], b_view[q, :, :])
+        bias_cols = held.tile([P, SQUARE], F32, name="bias_cols", align_bytes=64)
+        nc.vector.transpose(bias_cols[:], bias_rows[:])
 
         zeros = held.tile([P, WARM_COLUMNS], BF16, name="zeros")
         nc.vector.memset(zeros[:], 0.0)

import concourse.mybir as mybir
from concourse.masks import make_identity

F32 = mybir.dt.float32
BF16 = mybir.dt.bfloat16
U16 = mybir.dt.uint16
MULT = mybir.AluOpType.mult
ADD = mybir.AluOpType.add
SUBTRACT = mybir.AluOpType.subtract
IDENTITY = mybir.ActivationFunctionType.Identity

P = 128
H = 768
KB = H // P
KC = 2
T = 256
S = 1024
N = 2 * T
M = 1024
MB = M // P
SQUARE = 32
WARM_COLUMNS = 512
WARM_PRODUCTS = 6

FLOPS = 2 * H * M * T


def tile_globalpointermodel_kernel(tc, tab, hid, w, b, offs, out):
    nc = tc.nc
    with (
        tc.tile_pool(name="held", bufs=1) as held,
        tc.tile_pool(name="work", bufs=2) as work,
        tc.psum_pool(name="small_banks", bufs=1) as small_banks,
        tc.psum_pool(name="banks", bufs=1) as banks,
        tc.psum_pool(name="sum_banks", bufs=1) as sum_banks,
    ):
        bias_rows = held.tile([P, SQUARE], F32, name="bias_rows", align_bytes=64)
        nc.vector.memset(bias_rows[:], 0.0)
        b_view = b.rearrange("(m q i) one -> q m (i one)", q=P // SQUARE, i=SQUARE)
        for q in range(P // SQUARE):
            nc.scalar.dma_start(bias_rows[q * SQUARE : q * SQUARE + MB, :], b_view[q, :, :])
        bias_cols = held.tile([P, SQUARE], F32, name="bias_cols", align_bytes=64)
        nc.vector.transpose(bias_cols[:], bias_rows[:])

        zeros = held.tile([P, WARM_COLUMNS], BF16, name="zeros")
        nc.vector.memset(zeros[:], 0.0)
        warm_ps = small_banks.tile([P, WARM_COLUMNS], F32, name="warm_ps")
        for i in range(WARM_PRODUCTS):
            nc.tensor.matmul(warm_ps[:], zeros[:, 0:P], zeros[:], start=True, stop=True)

        offsets = held.tile([P, N // 16], U16, name="offsets")
        nc.sync.dma_start(offsets[:], offs)

        hid_sb = held.tile([P, KB, T], BF16, name="hid_sb")
        nc.sync.dma_start(hid_sb[:], hid.rearrange("(p k) t -> p k t", k=KB))

        w_view = w.rearrange("(p k) m -> p k m", k=KB)
        w_part = [
            [held.tile([P, KC, M // 2], BF16, name=f"w_part{h}_{i}") for i in range(KB // KC)] for h in range(2)
        ]
        table = [held.tile([P, S], F32, name=f"table{q}") for q in range(4)]

        def load_w(h):
            for i in range(KB // KC):
                nc.sync.dma_start(
                    w_part[h][i][:], w_view[:, i * KC : (i + 1) * KC, h * (M // 2) : (h + 1) * (M // 2)]
                )

        def load_table(q):
            nc.sync.dma_start(table[q][:], tab[q * P : (q + 1) * P, :])

        load_w(0)
        load_table(0)
        load_table(2)
        load_table(1)
        load_table(3)
        load_w(1)

        identity = held.tile([P, P], F32, name="identity")
        make_identity(nc, identity[:])
        minus_identity = held.tile([P, P], F32, name="minus_identity")
        nc.scalar.mul(minus_identity[:], identity[:], -1.0)

        def project_pair(h, g):
            accs = [banks.tile([P, T], F32, name=f"acc{member}") for member in range(2)]
            for k in range(KB):
                for member in range(2):
                    c = 2 * member + g
                    nc.tensor.matmul(
                        accs[member][:],
                        w_part[h][k // KC][:, k % KC, c * P : (c + 1) * P],
                        hid_sb[:, k, :],
                        start=(k == 0),
                        stop=(k == KB - 1),
                    )
            members = []
            for member in range(2):
                m = h * (MB // 2) + 2 * member + g
                v = work.tile([P, T], F32, name=f"v{member}")
                nc.scalar.activation(v[:], accs[member][:], IDENTITY, bias=bias_cols[:, m : m + 1])
                members.append(v)
            return members

        units = [(h, g) for h in range(2) for g in range(2)]
        projected = project_pair(*units[0])
        for u, (h, g) in enumerate(units):
            piece = offsets[:, h * (T // 16) : (h + 1) * (T // 16)]
            columns = slice(h * T, (h + 1) * T)
            cos, sin = table[g], table[2 + g]
            even, odd = projected
            if u + 1 < len(units):
                projected = project_pair(*units[u + 1])

            cos_even = work.tile([P, T], F32, name="cos_even")
            sin_odd = work.tile([P, T], F32, name="sin_odd")
            cos_odd = work.tile([P, T], F32, name="cos_odd")
            sin_even = work.tile([P, T], F32, name="sin_even")
            nc.vector.tensor_tensor(cos_even[:], cos[:].indirect(piece), even[:], MULT)
            nc.vector.tensor_tensor(cos_odd[:], cos[:].indirect(piece), odd[:], MULT)
            nc.vector.tensor_tensor(sin_odd[:], sin[:].indirect(piece), odd[:], MULT)
            nc.vector.tensor_tensor(sin_even[:], sin[:].indirect(piece), even[:], MULT)

            top = work.tile([P, T], F32, name="top")
            bottom = work.tile([P, T], F32, name="bottom")
            if g == 0:
                top_ps = sum_banks.tile([P, T], F32, name="top_ps")
                nc.tensor.matmul(top_ps[:], identity[:], cos_even[:], start=True, stop=False)
                nc.tensor.matmul(top_ps[:], minus_identity[:], sin_odd[:], start=False, stop=True)
                nc.scalar.activation(top[:], top_ps[:], IDENTITY)
            else:
                nc.vector.tensor_tensor(top[:], cos_even[:], sin_odd[:], SUBTRACT)
            nc.vector.tensor_tensor(bottom[:], cos_odd[:], sin_even[:], ADD)

            nc.sync.dma_start(out[g * P : (g + 1) * P, columns], top[:])
            nc.sync.dma_start(out[(2 + g) * P : (3 + g) * P, columns], bottom[:])
